import numpy as np
import ml_dtypes


def mxq(x, axis, fmt="e4m3"):
    dtype, down = {"e4m3": (ml_dtypes.float8_e4m3fn, 7), "e5m2": (ml_dtypes.float8_e5m2, 14)}[fmt]
    v = np.moveaxis(np.asarray(x, np.float32).astype(ml_dtypes.bfloat16).astype(np.float64), axis, -1)
    blocks = v.reshape(v.shape[:-1] + (-1, 32))
    amax = np.abs(blocks).max(-1, keepdims=True)
    byte = np.maximum(np.where(amax > 0, np.frexp(amax)[1] - 1 + 127, 0) - down, 1)
    scale = np.exp2(byte - 127.0)
    codes = (blocks / scale).astype(np.float32).astype(dtype).astype(np.float64)
    return np.moveaxis((codes * scale).reshape(v.shape), -1, axis)


WIDE = False


def mx_kscale(k):
    if not WIDE:
        return np.ones(k)
    levels = np.array([10, -10, 5, -5, 0])
    a = np.random.permutation(np.resize(levels, k // 512 * 4)).reshape(k // 512, 4)
    idx = np.arange(k)
    return np.exp2(a[idx // 512, idx % 128 // 32])


BF16 = ml_dtypes.bfloat16


def bf(x):
    return np.asarray(x, np.float32).astype(BF16)


def f64(x):
    return np.asarray(x).astype(np.float64)


B, N, W, H, D = 1, 16, 512, 4, 128
C = H * D


def setup_inputs():
    t = mx_kscale(C)
    return {"q_feat": bf(np.maximum(np.random.standard_normal((B, H, N, W, D)) * 0.5, 0.0)),
            "kv_mix": bf(np.random.standard_normal((B, H, N, D, D)) * 0.27 * np.sqrt(W / (2.0 * N)) * t.reshape(H, D)[None, :, None, None, :]),
            "w_out": bf(np.random.standard_normal((C, C)) * 0.5 / np.sqrt(C) / t[:, None]),
            "b_out": bf(np.random.standard_normal(C) * 0.3)}


def reference(q_feat, kv_mix, w_out, b_out):
    o = f64(q_feat) @ f64(kv_mix)
    o = o.transpose(0, 2, 3, 1, 4).reshape(B, N, W, C)
    return (mxq(o, 3, "e4m3") @ mxq(f64(w_out), 0, "e4m3")) + f64(b_out)

@@ -1,0 +1,147 @@
+from contextlib import ExitStack
+
+import concourse.mybir as mybir
+from concourse.masks import make_identity
+
+BF16 = mybir.dt.bfloat16
+F32 = mybir.dt.float32
+U32 = mybir.dt.uint32
+U8 = mybir.dt.uint8
+FP8X4 = mybir.dt.float8_e4m3fn_x4
+
+P = 128
+HEADS = 4
+WINDOWS = 16
+POSITIONS = 512
+HEAD_DIM = 128
+CHANNELS = HEADS * HEAD_DIM
+ROWS = POSITIONS // P
+KV_GROUP = 4
+MX_LAG = 3
+
+FLOPS = 2 * HEADS * WINDOWS * POSITIONS * HEAD_DIM * HEAD_DIM + 2 * WINDOWS * POSITIONS * CHANNELS * CHANNELS
+
+
+def tile_mhla_pb_t_kernel(tc, q_feat, kv_mix, w_out, b_out, out):
+    nc = tc.nc
+    with ExitStack() as ctx:
+        consts = ctx.enter_context(tc.tile_pool(name="consts", bufs=1))
+        q_pool = ctx.enter_context(tc.tile_pool(name="q_pool", bufs=WINDOWS))
+        kv_pool = ctx.enter_context(tc.tile_pool(name="kv_pool", bufs=WINDOWS // KV_GROUP))
+        work = ctx.enter_context(tc.tile_pool(name="work", bufs=3))
+        out_pool = ctx.enter_context(tc.tile_pool(name="out_pool", bufs=8))
+        t_psum = ctx.enter_context(tc.psum_pool(name="t_psum", bufs=2))
+        o_psum = ctx.enter_context(tc.psum_pool(name="o_psum", bufs=3))
+        r_psum = ctx.enter_context(tc.psum_pool(name="r_psum", bufs=3))
+        ctx.enter_context(tc.manual_schedule())
+
+        ident = consts.tile([P, P], BF16, name="ident")
+        make_identity(nc, ident[:])
+        ones = consts.tile([P, P], BF16, name="ones")
+        nc.vector.memset(ones[:], 1.0)
+        bias_rows = consts.tile([P, CHANNELS], BF16, name="bias_rows")
+        nc.vector.memset(bias_rows[:], 0.0)
+        nc.scalar.dma_start(out=bias_rows[0:1, :], in_=b_out.rearrange("(o c) -> o c", o=1))
+
+        w_raw = consts.tile([P, HEADS, CHANNELS], BF16, name="w_raw")
+        q_tiles = []
+        kv_tiles = []
+        for n in range(WINDOWS):
+            q_sb = q_pool.tile([P, HEADS, ROWS, HEAD_DIM], BF16, name="q_sb")
+            nc.sync.dma_start(
+                out=q_sb[:].rearrange("p h r d -> p h (r d)"),
+                in_=q_feat[0, :, n].rearrange("h (p r) d -> p h (r d)", r=ROWS),
+            )
+            q_tiles.append(q_sb)
+            if n % KV_GROUP == 0:
+                kv_sb = kv_pool.tile([P, HEADS, KV_GROUP, HEAD_DIM], BF16, name="kv_sb")
+                for h in range(HEADS):
+                    nc.sync.dma_start(
+                        out=kv_sb[:, h, :, :],
+                        in_=kv_mix[0, h, n : n + KV_GROUP].rearrange("n d e -> d n e"),
+                    )
+                kv_tiles.append(kv_sb)
+            if n == 0:
+                nc.sync.dma_start(out=w_raw[:], in_=w_out.rearrange("(t p) c -> p t c", p=P))
+
+        bias_ps = r_psum.tile([P, CHANNELS], F32, name="bias_ps", tag="r_bank")
+        nc.tensor.matmul(out=bias_ps[:], lhsT=ones[:], rhs=bias_rows[:], start=True, stop=True)
+        bias_sb = consts.tile([P, CHANNELS], F32, name="bias_sb")
+        nc.vector.tensor_copy(out=bias_sb[:], in_=bias_ps[:])
+
+        w_grouped = consts.tile([P, CHANNELS, HEADS], BF16, name="w_grouped", align_bytes=64)
+        nc.vector.tensor_copy(out=w_grouped[:], in_=w_raw[:].rearrange("p t c -> p c t"))
+        w_codes = consts.tile([P, CHANNELS], U32, name="w_codes", align_bytes=64)
+        w_scales = consts.tile([P, CHANNELS], U8, name="w_scales", align_bytes=64)
+        nc.vector.quantize_mx(
+            out=w_codes[:].bitcast(FP8X4),
+            scales=w_scales[:],
+            in_=w_grouped[:].rearrange("p c t -> p (c t)"),
+        )
+
+        q_transposed = {}
+        m_codes = {}
+        m_scales = {}
+
+        def transpose_window(n):
+            qT = work.tile([P, ROWS, HEADS, P], BF16, name="qT")
+            for half in range(2):
+                t_bank = t_psum.tile([P, 2, HEADS, P], BF16, name="t_bank")
+                for j in range(2):
+                    for h in range(HEADS):
+                        nc.tensor.transpose(t_bank[:, j, h, :], q_tiles[n][:, h, 2 * half + j, :], ident[:])
+                nc.scalar.copy(out=qT[:, 2 * half : 2 * half + 2, :, :], in_=t_bank[:])
+            q_transposed[n] = qT
+
+        def readout_window(n):
+            qT = q_transposed[n]
+            kv_sb = kv_tiles[n // KV_GROUP]
+            grouped = work.tile([P, ROWS, P, HEADS], BF16, name="grouped", align_bytes=64)
+            for r in range(ROWS):
+                o_bank = o_psum.tile([P, HEADS, P], F32, name="o_bank")
+                for h in range(HEADS):
+                    nc.tensor.matmul(
+                        out=o_bank[:, h, :],
+                        lhsT=kv_sb[:, h, n % KV_GROUP, :],
+                        rhs=qT[:, r, h, :],
+                        start=True,
+                        stop=True,
+                    )
+                nc.scalar.copy(out=grouped[:, r, :, :], in_=o_bank[:].rearrange("e t p -> e p t"))
+            codes = work.tile([P, ROWS * P], U32, name="codes", align_bytes=64)
+            scales = work.tile([P, ROWS * P], U8, name="scales", align_bytes=64)
+            nc.vector.quantize_mx(
+                out=codes[:].bitcast(FP8X4),
+                scales=scales[:],
+                in_=grouped[:].rearrange("e r p t -> e (r p t)"),
+            )
+            m_codes[n] = codes
+            m_scales[n] = scales
+
+        def project_window(n):
+            codes = m_codes[n]
+            scales = m_scales[n]
+            out_sb = out_pool.tile([P, ROWS, CHANNELS], F32, name="out_sb")
+            for r in range(ROWS):
+                r_bank = r_psum.tile([P, CHANNELS], F32, name="r_bank", tag="r_bank")
+                nc.tensor.matmul_mx(
+                    out=r_bank[:],
+                    lhsT=codes[:, r * P : (r + 1) * P].bitcast(FP8X4),
+                    lhsT_scale=scales[:, r * P : (r + 1) * P],
+                    rhs=w_codes[:].bitcast(FP8X4),
+                    rhs_scale=w_scales[:],
+                    start=True,
+                    stop=True,
+                )
+                nc.vector.tensor_tensor(
+                    out=out_sb[:, r, :], in0=r_bank[:], in1=bias_sb[:], op=mybir.AluOpType.add
+                )
+            nc.sync.dma_start(out=out[0, n].rearrange("(p r) c -> p r c", r=ROWS), in_=out_sb[:])
+
+        for step in range(WINDOWS + MX_LAG):
+            if step < WINDOWS:
+                transpose_window(step)
+            if step >= MX_LAG:
+                project_window(step - MX_LAG)
+            if 1 <= step <= WINDOWS:
+                readout_window(step - 1)

@@ -16,7 +16,9 @@ POSITIONS = 512
 HEAD_DIM = 128
 CHANNELS = HEADS * HEAD_DIM
 ROWS = POSITIONS // P
-KV_GROUP = 4
+HALVES = 2
+HALF_ROWS = ROWS // HALVES
+HALF = HALF_ROWS * P
 MX_LAG = 3
 
 FLOPS = 2 * HEADS * WINDOWS * POSITIONS * HEAD_DIM * HEAD_DIM + 2 * WINDOWS * POSITIONS * CHANNELS * CHANNELS
@@ -26,108 +28,114 @@ def tile_mhla_pb_t_kernel(tc, q_feat, kv_mix, w_out, b_out, out):
     nc = tc.nc
     with ExitStack() as ctx:
         consts = ctx.enter_context(tc.tile_pool(name="consts", bufs=1))
-        q_pool = ctx.enter_context(tc.tile_pool(name="q_pool", bufs=WINDOWS))
-        kv_pool = ctx.enter_context(tc.tile_pool(name="kv_pool", bufs=WINDOWS // KV_GROUP))
-        work = ctx.enter_context(tc.tile_pool(name="work", bufs=3))
+        inputs = ctx.enter_context(tc.tile_pool(name="inputs", bufs=WINDOWS))
+        short = ctx.enter_context(tc.tile_pool(name="short", bufs=3 * HALVES))
+        waiting = ctx.enter_context(tc.tile_pool(name="waiting", bufs=(MX_LAG + 1) * HALVES))
         out_pool = ctx.enter_context(tc.tile_pool(name="out_pool", bufs=8))
-        t_psum = ctx.enter_context(tc.psum_pool(name="t_psum", bufs=2))
-        o_psum = ctx.enter_context(tc.psum_pool(name="o_psum", bufs=3))
-        r_psum = ctx.enter_context(tc.psum_pool(name="r_psum", bufs=3))
+        t_psum = ctx.enter_context(tc.psum_pool(name="t_psum", bufs=HALVES))
+        o_psum = ctx.enter_context(tc.psum_pool(name="o_psum", bufs=HALVES))
+        r_psum = ctx.enter_context(tc.psum_pool(name="r_psum", bufs=ROWS))
         ctx.enter_context(tc.manual_schedule())
 
-        ident = consts.tile([P, P], BF16, name="ident")
-        make_identity(nc, ident[:])
-        ones = consts.tile([P, P], BF16, name="ones")
-        nc.vector.memset(ones[:], 1.0)
-        bias_rows = consts.tile([P, CHANNELS], BF16, name="bias_rows")
-        nc.vector.memset(bias_rows[:], 0.0)
-        nc.scalar.dma_start(out=bias_rows[0:1, :], in_=b_out.rearrange("(o c) -> o c", o=1))
-
-        w_raw = consts.tile([P, HEADS, CHANNELS], BF16, name="w_raw")
         q_tiles = []
         kv_tiles = []
+        w_raw = consts.tile([P, HEADS, CHANNELS], BF16, name="w_raw")
+        bias_rows = consts.tile([P, CHANNELS], BF16, name="bias_rows")
+        nc.vector.memset(bias_rows[:], 0.0)
         for n in range(WINDOWS):
-            q_sb = q_pool.tile([P, HEADS, ROWS, HEAD_DIM], BF16, name="q_sb")
+            q_sb = inputs.tile([P, HEADS, ROWS, HEAD_DIM], BF16, name="q_sb")
             nc.sync.dma_start(
                 out=q_sb[:].rearrange("p h r d -> p h (r d)"),
                 in_=q_feat[0, :, n].rearrange("h (p r) d -> p h (r d)", r=ROWS),
             )
             q_tiles.append(q_sb)
-            if n % KV_GROUP == 0:
-                kv_sb = kv_pool.tile([P, HEADS, KV_GROUP, HEAD_DIM], BF16, name="kv_sb")
-                for h in range(HEADS):
-                    nc.sync.dma_start(
-                        out=kv_sb[:, h, :, :],
-                        in_=kv_mix[0, h, n : n + KV_GROUP].rearrange("n d e -> d n e"),
-                    )
-                kv_tiles.append(kv_sb)
-            if n == 0:
-                nc.sync.dma_start(out=w_raw[:], in_=w_out.rearrange("(t p) c -> p t c", p=P))
+            kv_sb = inputs.tile([P, HEADS, HEAD_DIM], BF16, name="kv_sb")
+            nc.sync.dma_start(out=kv_sb[:], in_=kv_mix[0, :, n].rearrange("h d e -> d h e"))
+            kv_tiles.append(kv_sb)
+            if n == 1:
+                nc.sync.dma_start(out=w_raw[:], in_=w_out.rearrange("(t e) c -> e t c", e=P))
+                nc.sync.dma_start(out=bias_rows[0:1, :], in_=b_out.rearrange("(o c) -> o c", o=1))
 
-        bias_ps = r_psum.tile([P, CHANNELS], F32, name="bias_ps", tag="r_bank")
-        nc.tensor.matmul(out=bias_ps[:], lhsT=ones[:], rhs=bias_rows[:], start=True, stop=True)
-        bias_sb = consts.tile([P, CHANNELS], F32, name="bias_sb")
-        nc.vector.tensor_copy(out=bias_sb[:], in_=bias_ps[:])
+        ident = consts.tile([P, P], BF16, name="ident")
+        make_identity(nc, ident[:])
+        ones = consts.tile([P, P], BF16, name="ones")
+        nc.vector.memset(ones[:], 1.0)
 
-        w_grouped = consts.tile([P, CHANNELS, HEADS], BF16, name="w_grouped", align_bytes=64)
-        nc.vector.tensor_copy(out=w_grouped[:], in_=w_raw[:].rearrange("p t c -> p c t"))
         w_codes = consts.tile([P, CHANNELS], U32, name="w_codes", align_bytes=64)
         w_scales = consts.tile([P, CHANNELS], U8, name="w_scales", align_bytes=64)
-        nc.vector.quantize_mx(
-            out=w_codes[:].bitcast(FP8X4),
-            scales=w_scales[:],
-            in_=w_grouped[:].rearrange("p c t -> p (c t)"),
-        )
+        bias_sb = consts.tile([P, CHANNELS], F32, name="bias_sb")
+
+        def prepare_projection():
+            w_grouped = consts.tile([P, CHANNELS, HEADS], BF16, name="w_grouped", align_bytes=64)
+            nc.vector.tensor_copy(out=w_grouped[:], in_=w_raw[:].rearrange("e t c -> e c t"))
+            nc.vector.quantize_mx(
+                out=w_codes[:].bitcast(FP8X4),
+                scales=w_scales[:],
+                in_=w_grouped[:].rearrange("e c t -> e (c t)"),
+            )
+            bias_ps = r_psum.tile([P, CHANNELS], F32, name="bias_ps", tag="r_bank")
+            nc.tensor.matmul(out=bias_ps[:], lhsT=ones[:], rhs=bias_rows[:], start=True, stop=True)
+            nc.vector.tensor_copy(out=bias_sb[:], in_=bias_ps[:])
 
         q_transposed = {}
+        m_grouped = {}
         m_codes = {}
         m_scales = {}
 
-        def transpose_window(n):
-            qT = work.tile([P, ROWS, HEADS, P], BF16, name="qT")
-            for half in range(2):
-                t_bank = t_psum.tile([P, 2, HEADS, P], BF16, name="t_bank")
-                for j in range(2):
-                    for h in range(HEADS):
-                        nc.tensor.transpose(t_bank[:, j, h, :], q_tiles[n][:, h, 2 * half + j, :], ident[:])
-                nc.scalar.copy(out=qT[:, 2 * half : 2 * half + 2, :, :], in_=t_bank[:])
-            q_transposed[n] = qT
-
-        def readout_window(n):
-            qT = q_transposed[n]
-            kv_sb = kv_tiles[n // KV_GROUP]
-            grouped = work.tile([P, ROWS, P, HEADS], BF16, name="grouped", align_bytes=64)
-            for r in range(ROWS):
-                o_bank = o_psum.tile([P, HEADS, P], F32, name="o_bank")
+        def readout_and_transpose(n_read, n_next):
+            for half in range(HALVES):
+                if n_read is not None:
+                    o_bank = o_psum.tile([P, HEADS, HALF], BF16, name="o_bank")
+                if n_next is not None:
+                    t_bank = t_psum.tile([P, HEADS, HALF_ROWS, P], BF16, name="t_bank")
                 for h in range(HEADS):
-                    nc.tensor.matmul(
-                        out=o_bank[:, h, :],
-                        lhsT=kv_sb[:, h, n % KV_GROUP, :],
-                        rhs=qT[:, r, h, :],
-                        start=True,
-                        stop=True,
-                    )
-                nc.scalar.copy(out=grouped[:, r, :, :], in_=o_bank[:].rearrange("e t p -> e p t"))
-            codes = work.tile([P, ROWS * P], U32, name="codes", align_bytes=64)
-            scales = work.tile([P, ROWS * P], U8, name="scales", align_bytes=64)
-            nc.vector.quantize_mx(
-                out=codes[:].bitcast(FP8X4),
-                scales=scales[:],
-                in_=grouped[:].rearrange("e r p t -> e (r p t)"),
-            )
-            m_codes[n] = codes
-            m_scales[n] = scales
+                    if n_read is not None:
+                        nc.tensor.matmul(
+                            out=o_bank[:, h, :],
+                            lhsT=kv_tiles[n_read][:, h, :],
+                            rhs=q_transposed[n_read, half][:, h, :],
+                            start=True,
+                            stop=True,
+                        )
+                    if n_next is not None:
+                        for j in range(HALF_ROWS):
+                            nc.tensor.transpose(
+                                t_bank[:, h, j, :], q_tiles[n_next][:, h, half * HALF_ROWS + j, :], ident[:]
+                            )
+                if n_next is not None:
+                    qT = short.tile([P, HEADS, HALF], BF16, name="qT")
+                    if half == 0:
+                        nc.vector.tensor_copy(out=qT[:], in_=t_bank[:].rearrange("d h j p -> d h (j p)"))
+                    else:
+                        nc.scalar.copy(out=qT[:], in_=t_bank[:].rearrange("d h j p -> d h (j p)"))
+                    q_transposed[n_next, half] = qT
+                if n_read is not None:
+                    grouped = short.tile([P, HALF, HEADS], BF16, name="grouped", align_bytes=64)
+                    nc.scalar.copy(out=grouped[:], in_=o_bank[:].rearrange("e t c -> e c t"))
+                    m_grouped[n_read, half] = grouped
+
+        def quantise_window(n):
+            for half in range(HALVES):
+                codes = waiting.tile([P, HALF], U32, name="codes", align_bytes=64)
+                scales = waiting.tile([P, HALF], U8, name="scales", align_bytes=64)
+                nc.vector.quantize_mx(
+                    out=codes[:].bitcast(FP8X4),
+                    scales=scales[:],
+                    in_=m_grouped[n, half][:].rearrange("e c t -> e (c t)"),
+                )
+                m_codes[n, half] = codes
+                m_scales[n, half] = scales
 
         def project_window(n):
-            codes = m_codes[n]
-            scales = m_scales[n]
             out_sb = out_pool.tile([P, ROWS, CHANNELS], F32, name="out_sb")
             for r in range(ROWS):
+                half = r // HALF_ROWS
+                cols = slice((r % HALF_ROWS) * P, (r % HALF_ROWS + 1) * P)
                 r_bank = r_psum.tile([P, CHANNELS], F32, name="r_bank", tag="r_bank")
                 nc.tensor.matmul_mx(
                     out=r_bank[:],
-                    lhsT=codes[:, r * P : (r + 1) * P].bitcast(FP8X4),
-                    lhsT_scale=scales[:, r * P : (r + 1) * P],
+                    lhsT=m_codes[n, half][:, cols].bitcast(FP8X4),
+                    lhsT_scale=m_scales[n, half][:, cols],
                     rhs=w_codes[:].bitcast(FP8X4),
                     rhs_scale=w_scales[:],
                     start=True,
@@ -139,9 +147,13 @@ def tile_mhla_pb_t_kernel(tc, q_feat, kv_mix, w_out, b_out, out):
             nc.sync.dma_start(out=out[0, n].rearrange("(p r) c -> p r c", r=ROWS), in_=out_sb[:])
 
         for step in range(WINDOWS + MX_LAG):
-            if step < WINDOWS:
-                transpose_window(step)
+            n_next = step if step < WINDOWS else None
+            n_read = step - 1 if 1 <= step <= WINDOWS else None
+            if n_next is not None or n_read is not None:
+                readout_and_transpose(n_read, n_next)
+            if step == MX_LAG:
+                prepare_projection()
             if step >= MX_LAG:
                 project_window(step - MX_LAG)
-            if 1 <= step <= WINDOWS:
-                readout_window(step - 1)
+            if n_read is not None:
+                quantise_window(n_read)

@@ -30,8 +30,8 @@ def tile_mhla_pb_t_kernel(tc, q_feat, kv_mix, w_out, b_out, out):
         consts = ctx.enter_context(tc.tile_pool(name="consts", bufs=1))
         inputs = ctx.enter_context(tc.tile_pool(name="inputs", bufs=WINDOWS))
         short = ctx.enter_context(tc.tile_pool(name="short", bufs=3 * HALVES))
-        waiting = ctx.enter_context(tc.tile_pool(name="waiting", bufs=(MX_LAG + 1) * HALVES))
-        out_pool = ctx.enter_context(tc.tile_pool(name="out_pool", bufs=8))
+        waiting = ctx.enter_context(tc.tile_pool(name="waiting", bufs=MX_LAG + 1))
+        out_pool = ctx.enter_context(tc.tile_pool(name="out_pool", bufs=8 * HALVES))
         t_psum = ctx.enter_context(tc.psum_pool(name="t_psum", bufs=HALVES))
         o_psum = ctx.enter_context(tc.psum_pool(name="o_psum", bufs=HALVES))
         r_psum = ctx.enter_context(tc.psum_pool(name="r_psum", bufs=ROWS))
@@ -82,76 +82,85 @@ def tile_mhla_pb_t_kernel(tc, q_feat, kv_mix, w_out, b_out, out):
         m_codes = {}
         m_scales = {}
 
+        def readout(n, half, h, o_bank):
+            nc.tensor.matmul(
+                out=o_bank[:, h, :],
+                lhsT=kv_tiles[n][:, h, :],
+                rhs=q_transposed[n, half][:, h, :],
+                start=True,
+                stop=True,
+            )
+
+        def transpose_pair(n, half, h, t_bank):
+            for j in range(HALF_ROWS):
+                nc.tensor.transpose(t_bank[:, h, j, :], q_tiles[n][:, h, half * HALF_ROWS + j, :], ident[:])
+
         def readout_and_transpose(n_read, n_next):
+            if n_read is not None:
+                grouped = short.tile([P, HALVES, HALF, HEADS], BF16, name="grouped", align_bytes=64)
+                m_grouped[n_read] = grouped
             for half in range(HALVES):
                 if n_read is not None:
                     o_bank = o_psum.tile([P, HEADS, HALF], BF16, name="o_bank")
                 if n_next is not None:
                     t_bank = t_psum.tile([P, HEADS, HALF_ROWS, P], BF16, name="t_bank")
                 for h in range(HEADS):
-                    if n_read is not None:
-                        nc.tensor.matmul(
-                            out=o_bank[:, h, :],
-                            lhsT=kv_tiles[n_read][:, h, :],
-                            rhs=q_transposed[n_read, half][:, h, :],
-                            start=True,
-                            stop=True,
-                        )
+                    if n_read is not None and half == 0:
+                        readout(n_read, half, h, o_bank)
                     if n_next is not None:
-                        for j in range(HALF_ROWS):
-                            nc.tensor.transpose(
-                                t_bank[:, h, j, :], q_tiles[n_next][:, h, half * HALF_ROWS + j, :], ident[:]
-                            )
+                        transpose_pair(n_next, half, h, t_bank)
+                    if n_read is not None and half == 1:
+                        readout(n_read, half, h, o_bank)
                 if n_next is not None:
                     qT = short.tile([P, HEADS, HALF], BF16, name="qT")
-                    if half == 0:
+                    if n_next < MX_LAG or (half == 0 and n_next % 2 == 0):
                         nc.vector.tensor_copy(out=qT[:], in_=t_bank[:].rearrange("d h j p -> d h (j p)"))
                     else:
                         nc.scalar.copy(out=qT[:], in_=t_bank[:].rearrange("d h j p -> d h (j p)"))
                     q_transposed[n_next, half] = qT
                 if n_read is not None:
-                    grouped = short.tile([P, HALF, HEADS], BF16, name="grouped", align_bytes=64)
-                    nc.scalar.copy(out=grouped[:], in_=o_bank[:].rearrange("e t c -> e c t"))
-                    m_grouped[n_read, half] = grouped
+                    nc.scalar.copy(out=grouped[:, half, :, :], in_=o_bank[:].rearrange("e t c -> e c t"))
 
         def quantise_window(n):
-            for half in range(HALVES):
-                codes = waiting.tile([P, HALF], U32, name="codes", align_bytes=64)
-                scales = waiting.tile([P, HALF], U8, name="scales", align_bytes=64)
-                nc.vector.quantize_mx(
-                    out=codes[:].bitcast(FP8X4),
-                    scales=scales[:],
-                    in_=m_grouped[n, half][:].rearrange("e c t -> e (c t)"),
-                )
-                m_codes[n, half] = codes
-                m_scales[n, half] = scales
+            codes = waiting.tile([P, POSITIONS], U32, name="codes", align_bytes=64)
+            scales = waiting.tile([P, POSITIONS], U8, name="scales", align_bytes=64)
+            nc.vector.quantize_mx(
+                out=codes[:].bitcast(FP8X4),
+                scales=scales[:],
+                in_=m_grouped[n][:].rearrange("e f c t -> e (f c t)"),
+            )
+            m_codes[n] = codes
+            m_scales[n] = scales
 
         def project_window(n):
-            out_sb = out_pool.tile([P, ROWS, CHANNELS], F32, name="out_sb")
-            for r in range(ROWS):
-                half = r // HALF_ROWS
-                cols = slice((r % HALF_ROWS) * P, (r % HALF_ROWS + 1) * P)
-                r_bank = r_psum.tile([P, CHANNELS], F32, name="r_bank", tag="r_bank")
-                nc.tensor.matmul_mx(
-                    out=r_bank[:],
-                    lhsT=m_codes[n, half][:, cols].bitcast(FP8X4),
-                    lhsT_scale=m_scales[n, half][:, cols],
-                    rhs=w_codes[:].bitcast(FP8X4),
-                    rhs_scale=w_scales[:],
-                    start=True,
-                    stop=True,
+            for half in range(HALVES):
+                out_sb = out_pool.tile([P, HALF_ROWS, CHANNELS], F32, name="out_sb")
+                for j in range(HALF_ROWS):
+                    r = half * HALF_ROWS + j
+                    r_bank = r_psum.tile([P, CHANNELS], F32, name="r_bank", tag="r_bank")
+                    nc.tensor.matmul_mx(
+                        out=r_bank[:],
+                        lhsT=m_codes[n][:, r * P : (r + 1) * P].bitcast(FP8X4),
+                        lhsT_scale=m_scales[n][:, r * P : (r + 1) * P],
+                        rhs=w_codes[:].bitcast(FP8X4),
+                        rhs_scale=w_scales[:],
+                        start=True,
+                        stop=True,
+                    )
+                    nc.vector.tensor_tensor(
+                        out=out_sb[:, j, :], in0=r_bank[:], in1=bias_sb[:], op=mybir.AluOpType.add
+                    )
+                rows = slice(half * HALF_ROWS, (half + 1) * HALF_ROWS)
+                nc.sync.dma_start(
+                    out=out[0, n].rearrange("(p r) c -> p r c", r=ROWS)[:, rows, :], in_=out_sb[:]
                 )
-                nc.vector.tensor_tensor(
-                    out=out_sb[:, r, :], in0=r_bank[:], in1=bias_sb[:], op=mybir.AluOpType.add
-                )
-            nc.sync.dma_start(out=out[0, n].rearrange("(p r) c -> p r c", r=ROWS), in_=out_sb[:])
 
         for step in range(WINDOWS + MX_LAG):
             n_next = step if step < WINDOWS else None
             n_read = step - 1 if 1 <= step <= WINDOWS else None
             if n_next is not None or n_read is not None:
                 readout_and_transpose(n_read, n_next)
-            if step == MX_LAG:
+            if step == MX_LAG - 1:
                 prepare_projection()
             if step >= MX_LAG:
                 project_window(step - MX_LAG)

@@ -15,10 +15,15 @@ WINDOWS = 16
 POSITIONS = 512
 HEAD_DIM = 128
 CHANNELS = HEADS * HEAD_DIM
-ROWS = POSITIONS // P
-HALVES = 2
-HALF_ROWS = ROWS // HALVES
-HALF = HALF_ROWS * P
+GROUP = 2
+GROUPS = WINDOWS // GROUP
+GROUP_ROWS = GROUP * POSITIONS // P
+SHARE = P // GROUP
+UNIT_ROWS = 4
+GROUP_UNITS = GROUP_ROWS // UNIT_ROWS
+UNITS = GROUPS * GROUP_UNITS
+BANK_BLOCKS = 8
+BANK_HEADS = BANK_BLOCKS // UNIT_ROWS
 MX_LAG = 3
 
 FLOPS = 2 * HEADS * WINDOWS * POSITIONS * HEAD_DIM * HEAD_DIM + 2 * WINDOWS * POSITIONS * CHANNELS * CHANNELS
@@ -28,31 +33,40 @@ def tile_mhla_pb_t_kernel(tc, q_feat, kv_mix, w_out, b_out, out):
     nc = tc.nc
     with ExitStack() as ctx:
         consts = ctx.enter_context(tc.tile_pool(name="consts", bufs=1))
-        inputs = ctx.enter_context(tc.tile_pool(name="inputs", bufs=WINDOWS))
-        short = ctx.enter_context(tc.tile_pool(name="short", bufs=3 * HALVES))
+        q_pool = ctx.enter_context(tc.tile_pool(name="q_pool", bufs=GROUPS))
+        kv_pool = ctx.enter_context(tc.tile_pool(name="kv_pool", bufs=WINDOWS))
+        short = ctx.enter_context(tc.tile_pool(name="short", bufs=6))
         waiting = ctx.enter_context(tc.tile_pool(name="waiting", bufs=MX_LAG + 1))
-        out_pool = ctx.enter_context(tc.tile_pool(name="out_pool", bufs=8 * HALVES))
-        t_psum = ctx.enter_context(tc.psum_pool(name="t_psum", bufs=HALVES))
-        o_psum = ctx.enter_context(tc.psum_pool(name="o_psum", bufs=HALVES))
-        r_psum = ctx.enter_context(tc.psum_pool(name="r_psum", bufs=ROWS))
+        out_pool = ctx.enter_context(tc.tile_pool(name="out_pool", bufs=8))
+        t_psum = ctx.enter_context(tc.psum_pool(name="t_psum", bufs=2))
+        o_psum = ctx.enter_context(tc.psum_pool(name="o_psum", bufs=2))
+        r_psum = ctx.enter_context(tc.psum_pool(name="r_psum", bufs=4))
         ctx.enter_context(tc.manual_schedule())
 
+        q_rows = q_feat[0].rearrange("h n w d -> h (n w) d")
+        out_rows = out[0].rearrange("n w c -> (n w) c")
         q_tiles = []
         kv_tiles = []
         w_raw = consts.tile([P, HEADS, CHANNELS], BF16, name="w_raw")
         bias_rows = consts.tile([P, CHANNELS], BF16, name="bias_rows")
         nc.vector.memset(bias_rows[:], 0.0)
-        for n in range(WINDOWS):
-            q_sb = inputs.tile([P, HEADS, ROWS, HEAD_DIM], BF16, name="q_sb")
-            nc.sync.dma_start(
-                out=q_sb[:].rearrange("p h r d -> p h (r d)"),
-                in_=q_feat[0, :, n].rearrange("h (p r) d -> p h (r d)", r=ROWS),
+        for g in range(GROUPS):
+            q_sb = q_pool.tile([P, HEADS, GROUP_ROWS, HEAD_DIM], BF16, name="q_sb")
+            q_group = q_rows[:, g * GROUP * POSITIONS : (g + 1) * GROUP * POSITIONS, :].rearrange(
+                "h (p r) d -> p h r d", r=GROUP_ROWS
             )
+            if g == 0:
+                for u in range(GROUP_UNITS):
+                    rows = slice(u * UNIT_ROWS, (u + 1) * UNIT_ROWS)
+                    nc.sync.dma_start(out=q_sb[:, :, rows, :], in_=q_group[:, :, rows, :])
+            else:
+                nc.sync.dma_start(out=q_sb[:], in_=q_group)
             q_tiles.append(q_sb)
-            kv_sb = inputs.tile([P, HEADS, HEAD_DIM], BF16, name="kv_sb")
-            nc.sync.dma_start(out=kv_sb[:], in_=kv_mix[0, :, n].rearrange("h d e -> d h e"))
-            kv_tiles.append(kv_sb)
-            if n == 1:
+            for a in range(GROUP):
+                kv_sb = kv_pool.tile([P, HEADS, HEAD_DIM], BF16, name="kv_sb")
+                nc.sync.dma_start(out=kv_sb[:], in_=kv_mix[0, :, g * GROUP + a].rearrange("h d e -> d h e"))
+                kv_tiles.append(kv_sb)
+            if g == 0:
                 nc.sync.dma_start(out=w_raw[:], in_=w_out.rearrange("(t e) c -> e t c", e=P))
                 nc.sync.dma_start(out=bias_rows[0:1, :], in_=b_out.rearrange("(o c) -> o c", o=1))
 
@@ -82,87 +96,97 @@ def tile_mhla_pb_t_kernel(tc, q_feat, kv_mix, w_out, b_out, out):
         m_codes = {}
         m_scales = {}
 
-        def readout(n, half, h, o_bank):
+        def readout(unit, a, h, o_bank):
+            qT = q_transposed[unit, h // BANK_HEADS]
+            blocks = qT[:].rearrange("d (s j p) -> d s j p", s=BANK_HEADS, j=UNIT_ROWS)
             nc.tensor.matmul(
-                out=o_bank[:, h, :],
-                lhsT=kv_tiles[n][:, h, :],
-                rhs=q_transposed[n, half][:, h, :],
+                out=o_bank[:, h, :, :],
+                lhsT=kv_tiles[unit // GROUP_UNITS * GROUP + a][:, h, :],
+                rhs=blocks[:, h % BANK_HEADS, :, a * SHARE : (a + 1) * SHARE],
                 start=True,
                 stop=True,
             )
 
-        def transpose_pair(n, half, h, t_bank):
-            for j in range(HALF_ROWS):
-                nc.tensor.transpose(t_bank[:, h, j, :], q_tiles[n][:, h, half * HALF_ROWS + j, :], ident[:])
+        def transpose_pair(unit, bank, k, t_bank):
+            for block in range(2 * k, 2 * k + 2):
+                h = bank * BANK_HEADS + block // UNIT_ROWS
+                r = unit % GROUP_UNITS * UNIT_ROWS + block % UNIT_ROWS
+                nc.tensor.transpose(
+                    t_bank[:, block * P : (block + 1) * P], q_tiles[unit // GROUP_UNITS][:, h, r, :], ident[:]
+                )
 
-        def readout_and_transpose(n_read, n_next):
-            if n_read is not None:
-                grouped = short.tile([P, HALVES, HALF, HEADS], BF16, name="grouped", align_bytes=64)
-                m_grouped[n_read] = grouped
-            for half in range(HALVES):
-                if n_read is not None:
-                    o_bank = o_psum.tile([P, HEADS, HALF], BF16, name="o_bank")
-                if n_next is not None:
-                    t_bank = t_psum.tile([P, HEADS, HALF_ROWS, P], BF16, name="t_bank")
-                for h in range(HEADS):
-                    if n_read is not None and half == 0:
-                        readout(n_read, half, h, o_bank)
-                    if n_next is not None:
-                        transpose_pair(n_next, half, h, t_bank)
-                    if n_read is not None and half == 1:
-                        readout(n_read, half, h, o_bank)
-                if n_next is not None:
-                    qT = short.tile([P, HEADS, HALF], BF16, name="qT")
-                    if n_next < MX_LAG or (half == 0 and n_next % 2 == 0):
-                        nc.vector.tensor_copy(out=qT[:], in_=t_bank[:].rearrange("d h j p -> d h (j p)"))
+        def readout_and_transpose(unit_read, unit_next):
+            if unit_read is not None:
+                grouped = short.tile([P, UNIT_ROWS, P, HEADS], BF16, name="grouped", align_bytes=64)
+                m_grouped[unit_read] = grouped
+            for half in range(2):
+                if unit_read is not None:
+                    o_bank = o_psum.tile([P, HEADS, UNIT_ROWS, SHARE], BF16, name="o_bank")
+                if unit_next is not None:
+                    t_bank = t_psum.tile([P, BANK_BLOCKS * P], BF16, name="t_bank")
+                for k in range(HEADS):
+                    if unit_read is not None and half == 0:
+                        readout(unit_read, half, k, o_bank)
+                    if unit_next is not None:
+                        transpose_pair(unit_next, half, k, t_bank)
+                    if unit_read is not None and half == 1:
+                        readout(unit_read, half, k, o_bank)
+                if unit_next is not None:
+                    qT = short.tile([P, BANK_BLOCKS * P], BF16, name="qT")
+                    if unit_next < MX_LAG or (half == 0 and unit_next % 2 == 0):
+                        nc.vector.tensor_copy(out=qT[:].bitcast(F32), in_=t_bank[:].bitcast(F32))
                     else:
-                        nc.scalar.copy(out=qT[:], in_=t_bank[:].rearrange("d h j p -> d h (j p)"))
-                    q_transposed[n_next, half] = qT
-                if n_read is not None:
-                    nc.scalar.copy(out=grouped[:, half, :, :], in_=o_bank[:].rearrange("e t c -> e c t"))
+                        nc.scalar.copy(out=qT[:].bitcast(F32), in_=t_bank[:].bitcast(F32))
+                    q_transposed[unit_next, half] = qT
+                if unit_read is not None:
+                    nc.scalar.copy(
+                        out=grouped[:, :, half * SHARE : (half + 1) * SHARE, :],
+                        in_=o_bank[:].rearrange("e t j i -> e j i t"),
+                    )
 
-        def quantise_window(n):
-            codes = waiting.tile([P, POSITIONS], U32, name="codes", align_bytes=64)
-            scales = waiting.tile([P, POSITIONS], U8, name="scales", align_bytes=64)
+        def quantise_unit(unit):
+            codes = waiting.tile([P, UNIT_ROWS * P], U32, name="codes", align_bytes=64)
+            scales = waiting.tile([P, UNIT_ROWS * P], U8, name="scales", align_bytes=64)
             nc.vector.quantize_mx(
                 out=codes[:].bitcast(FP8X4),
                 scales=scales[:],
-                in_=m_grouped[n][:].rearrange("e f c t -> e (f c t)"),
+                in_=m_grouped[unit][:].rearrange("e j p t -> e (j p t)"),
             )
-            m_codes[n] = codes
-            m_scales[n] = scales
+            m_codes[unit] = codes
+            m_scales[unit] = scales
 
-        def project_window(n):
-            for half in range(HALVES):
-                out_sb = out_pool.tile([P, HALF_ROWS, CHANNELS], F32, name="out_sb")
-                for j in range(HALF_ROWS):
-                    r = half * HALF_ROWS + j
-                    r_bank = r_psum.tile([P, CHANNELS], F32, name="r_bank", tag="r_bank")
-                    nc.tensor.matmul_mx(
-                        out=r_bank[:],
-                        lhsT=m_codes[n][:, r * P : (r + 1) * P].bitcast(FP8X4),
-                        lhsT_scale=m_scales[n][:, r * P : (r + 1) * P],
-                        rhs=w_codes[:].bitcast(FP8X4),
-                        rhs_scale=w_scales[:],
-                        start=True,
-                        stop=True,
-                    )
-                    nc.vector.tensor_tensor(
-                        out=out_sb[:, j, :], in0=r_bank[:], in1=bias_sb[:], op=mybir.AluOpType.add
-                    )
-                rows = slice(half * HALF_ROWS, (half + 1) * HALF_ROWS)
-                nc.sync.dma_start(
-                    out=out[0, n].rearrange("(p r) c -> p r c", r=ROWS)[:, rows, :], in_=out_sb[:]
+        def project_unit(unit):
+            g = unit // GROUP_UNITS
+            u = unit % GROUP_UNITS
+            out_unit = out_rows[g * GROUP * POSITIONS : (g + 1) * GROUP * POSITIONS, :].rearrange(
+                "(p r) c -> p r c", r=GROUP_ROWS
+            )[:, u * UNIT_ROWS : (u + 1) * UNIT_ROWS, :]
+            store_rows = UNIT_ROWS // 2 if unit == UNITS - 1 else UNIT_ROWS
+            out_sb = out_pool.tile([P, UNIT_ROWS, CHANNELS], F32, name="out_sb")
+            for j in range(UNIT_ROWS):
+                r_bank = r_psum.tile([P, CHANNELS], F32, name="r_bank", tag="r_bank")
+                nc.tensor.matmul_mx(
+                    out=r_bank[:],
+                    lhsT=m_codes[unit][:, j * P : (j + 1) * P].bitcast(FP8X4),
+                    lhsT_scale=m_scales[unit][:, j * P : (j + 1) * P],
+                    rhs=w_codes[:].bitcast(FP8X4),
+                    rhs_scale=w_scales[:],
+                    start=True,
+                    stop=True,
                 )
+                nc.vector.tensor_tensor(out=out_sb[:, j, :], in0=r_bank[:], in1=bias_sb[:], op=mybir.AluOpType.add)
+                if (j + 1) % store_rows == 0:
+                    rows = slice(j + 1 - store_rows, j + 1)
+                    nc.sync.dma_start(out=out_unit[:, rows, :], in_=out_sb[:, rows, :])
 
-        for step in range(WINDOWS + MX_LAG):
-            n_next = step if step < WINDOWS else None
-            n_read = step - 1 if 1 <= step <= WINDOWS else None
-            if n_next is not None or n_read is not None:
-                readout_and_transpose(n_read, n_next)
+        for step in range(UNITS + MX_LAG):
+            unit_next = step if step < UNITS else None
+            unit_read = step - 1 if 1 <= step <= UNITS else None
+            if unit_next is not None or unit_read is not None:
+                readout_and_transpose(unit_read, unit_next)
             if step == MX_LAG - 1:
                 prepare_projection()
             if step >= MX_LAG:
-                project_window(step - MX_LAG)
-            if n_read is not None:
-                quantise_window(n_read)
+                project_unit(step - MX_LAG)
+            if unit_read is not None:
+                quantise_unit(unit_read)

@@ -161,7 +161,7 @@ def tile_mhla_pb_t_kernel(tc, q_feat, kv_mix, w_out, b_out, out):
             out_unit = out_rows[g * GROUP * POSITIONS : (g + 1) * GROUP * POSITIONS, :].rearrange(
                 "(p r) c -> p r c", r=GROUP_ROWS
             )[:, u * UNIT_ROWS : (u + 1) * UNIT_ROWS, :]
-            store_rows = UNIT_ROWS // 2 if unit == UNITS - 1 else UNIT_ROWS
+            store_rows = UNIT_ROWS // 2
             out_sb = out_pool.tile([P, UNIT_ROWS, CHANNELS], F32, name="out_sb")
             for j in range(UNIT_ROWS):
                 r_bank = r_psum.tile([P, CHANNELS], F32, name="r_bank", tag="r_bank")

@@ -17,14 +17,18 @@ HEAD_DIM = 128
 CHANNELS = HEADS * HEAD_DIM
 GROUP = 2
 GROUPS = WINDOWS // GROUP
-GROUP_ROWS = GROUP * POSITIONS // P
+GROUP_POSITIONS = GROUP * POSITIONS
+GROUP_ROWS = GROUP_POSITIONS // P
 SHARE = P // GROUP
 UNIT_ROWS = 4
 GROUP_UNITS = GROUP_ROWS // UNIT_ROWS
 UNITS = GROUPS * GROUP_UNITS
 BANK_BLOCKS = 8
 BANK_HEADS = BANK_BLOCKS // UNIT_ROWS
+UNIT_BANKS = 2
 MX_LAG = 3
+
+assert UNIT_BANKS == GROUP and UNIT_BANKS * BANK_HEADS == HEADS and BANK_BLOCKS == 2 * HEADS
 
 FLOPS = 2 * HEADS * WINDOWS * POSITIONS * HEAD_DIM * HEAD_DIM + 2 * WINDOWS * POSITIONS * CHANNELS * CHANNELS
 
@@ -35,12 +39,12 @@ def tile_mhla_pb_t_kernel(tc, q_feat, kv_mix, w_out, b_out, out):
         consts = ctx.enter_context(tc.tile_pool(name="consts", bufs=1))
         q_pool = ctx.enter_context(tc.tile_pool(name="q_pool", bufs=GROUPS))
         kv_pool = ctx.enter_context(tc.tile_pool(name="kv_pool", bufs=WINDOWS))
-        short = ctx.enter_context(tc.tile_pool(name="short", bufs=6))
+        short = ctx.enter_context(tc.tile_pool(name="short", bufs=3 * UNIT_BANKS))
         waiting = ctx.enter_context(tc.tile_pool(name="waiting", bufs=MX_LAG + 1))
-        out_pool = ctx.enter_context(tc.tile_pool(name="out_pool", bufs=8))
-        t_psum = ctx.enter_context(tc.psum_pool(name="t_psum", bufs=2))
-        o_psum = ctx.enter_context(tc.psum_pool(name="o_psum", bufs=2))
-        r_psum = ctx.enter_context(tc.psum_pool(name="r_psum", bufs=4))
+        out_pool = ctx.enter_context(tc.tile_pool(name="out_pool", bufs=UNITS // 2))
+        t_psum = ctx.enter_context(tc.psum_pool(name="t_psum", bufs=UNIT_BANKS))
+        o_psum = ctx.enter_context(tc.psum_pool(name="o_psum", bufs=UNIT_BANKS))
+        r_psum = ctx.enter_context(tc.psum_pool(name="r_psum", bufs=UNIT_ROWS))
         ctx.enter_context(tc.manual_schedule())
 
         q_rows = q_feat[0].rearrange("h n w d -> h (n w) d")
@@ -52,7 +56,7 @@ def tile_mhla_pb_t_kernel(tc, q_feat, kv_mix, w_out, b_out, out):
         nc.vector.memset(bias_rows[:], 0.0)
         for g in range(GROUPS):
             q_sb = q_pool.tile([P, HEADS, GROUP_ROWS, HEAD_DIM], BF16, name="q_sb")
-            q_group = q_rows[:, g * GROUP * POSITIONS : (g + 1) * GROUP * POSITIONS, :].rearrange(
+            q_group = q_rows[:, g * GROUP_POSITIONS : (g + 1) * GROUP_POSITIONS, :].rearrange(
                 "h (p r) d -> p h r d", r=GROUP_ROWS
             )
             if g == 0:
@@ -107,8 +111,8 @@ def tile_mhla_pb_t_kernel(tc, q_feat, kv_mix, w_out, b_out, out):
                 stop=True,
             )
 
-        def transpose_pair(unit, bank, k, t_bank):
-            for block in range(2 * k, 2 * k + 2):
+        def transpose_pair(unit, bank, turn, t_bank):
+            for block in range(2 * turn, 2 * turn + 2):
                 h = bank * BANK_HEADS + block // UNIT_ROWS
                 r = unit % GROUP_UNITS * UNIT_ROWS + block % UNIT_ROWS
                 nc.tensor.transpose(
@@ -119,28 +123,26 @@ def tile_mhla_pb_t_kernel(tc, q_feat, kv_mix, w_out, b_out, out):
             if unit_read is not None:
                 grouped = short.tile([P, UNIT_ROWS, P, HEADS], BF16, name="grouped", align_bytes=64)
                 m_grouped[unit_read] = grouped
-            for half in range(2):
+            for bank in range(UNIT_BANKS):
                 if unit_read is not None:
                     o_bank = o_psum.tile([P, HEADS, UNIT_ROWS, SHARE], BF16, name="o_bank")
                 if unit_next is not None:
                     t_bank = t_psum.tile([P, BANK_BLOCKS * P], BF16, name="t_bank")
-                for k in range(HEADS):
-                    if unit_read is not None and half == 0:
-                        readout(unit_read, half, k, o_bank)
+                for turn in range(HEADS):
+                    if unit_read is not None:
+                        readout(unit_read, bank, turn, o_bank)
                     if unit_next is not None:
-                        transpose_pair(unit_next, half, k, t_bank)
-                    if unit_read is not None and half == 1:
-                        readout(unit_read, half, k, o_bank)
+                        transpose_pair(unit_next, bank, turn, t_bank)
                 if unit_next is not None:
                     qT = short.tile([P, BANK_BLOCKS * P], BF16, name="qT")
-                    if unit_next < MX_LAG or (half == 0 and unit_next % 2 == 0):
+                    if unit_next < MX_LAG:
                         nc.vector.tensor_copy(out=qT[:].bitcast(F32), in_=t_bank[:].bitcast(F32))
                     else:
                         nc.scalar.copy(out=qT[:].bitcast(F32), in_=t_bank[:].bitcast(F32))
-                    q_transposed[unit_next, half] = qT
+                    q_transposed[unit_next, bank] = qT
                 if unit_read is not None:
                     nc.scalar.copy(
-                        out=grouped[:, :, half * SHARE : (half + 1) * SHARE, :],
+                        out=grouped[:, :, bank * SHARE : (bank + 1) * SHARE, :],
                         in_=o_bank[:].rearrange("e t j i -> e j i t"),
                     )
 
@@ -158,10 +160,9 @@ def tile_mhla_pb_t_kernel(tc, q_feat, kv_mix, w_out, b_out, out):
         def project_unit(unit):
             g = unit // GROUP_UNITS
             u = unit % GROUP_UNITS
-            out_unit = out_rows[g * GROUP * POSITIONS : (g + 1) * GROUP * POSITIONS, :].rearrange(
+            out_unit = out_rows[g * GROUP_POSITIONS : (g + 1) * GROUP_POSITIONS, :].rearrange(
                 "(p r) c -> p r c", r=GROUP_ROWS
             )[:, u * UNIT_ROWS : (u + 1) * UNIT_ROWS, :]
-            store_rows = UNIT_ROWS // 2
             out_sb = out_pool.tile([P, UNIT_ROWS, CHANNELS], F32, name="out_sb")
             for j in range(UNIT_ROWS):
                 r_bank = r_psum.tile([P, CHANNELS], F32, name="r_bank", tag="r_bank")
@@ -175,9 +176,7 @@ def tile_mhla_pb_t_kernel(tc, q_feat, kv_mix, w_out, b_out, out):
                     stop=True,
                 )
                 nc.vector.tensor_tensor(out=out_sb[:, j, :], in0=r_bank[:], in1=bias_sb[:], op=mybir.AluOpType.add)
-                if (j + 1) % store_rows == 0:
-                    rows = slice(j + 1 - store_rows, j + 1)
-                    nc.sync.dma_start(out=out_unit[:, rows, :], in_=out_sb[:, rows, :])
+            nc.sync.dma_start(out=out_unit, in_=out_sb[:])
 
         for step in range(UNITS + MX_LAG):
             unit_next = step if step < UNITS else None

from contextlib import ExitStack

import concourse.mybir as mybir
from concourse.masks import make_identity

BF16 = mybir.dt.bfloat16
F32 = mybir.dt.float32
U32 = mybir.dt.uint32
U8 = mybir.dt.uint8
FP8X4 = mybir.dt.float8_e4m3fn_x4

P = 128
HEADS = 4
WINDOWS = 16
POSITIONS = 512
HEAD_DIM = 128
CHANNELS = HEADS * HEAD_DIM
GROUP = 2
GROUPS = WINDOWS // GROUP
GROUP_POSITIONS = GROUP * POSITIONS
GROUP_ROWS = GROUP_POSITIONS // P
SHARE = P // GROUP
UNIT_ROWS = 4
GROUP_UNITS = GROUP_ROWS // UNIT_ROWS
UNITS = GROUPS * GROUP_UNITS
BANK_BLOCKS = 8
BANK_HEADS = BANK_BLOCKS // UNIT_ROWS
UNIT_BANKS = 2
MX_LAG = 3

assert UNIT_BANKS == GROUP and UNIT_BANKS * BANK_HEADS == HEADS and BANK_BLOCKS == 2 * HEADS

FLOPS = 2 * HEADS * WINDOWS * POSITIONS * HEAD_DIM * HEAD_DIM + 2 * WINDOWS * POSITIONS * CHANNELS * CHANNELS


def tile_mhla_pb_t_kernel(tc, q_feat, kv_mix, w_out, b_out, out):
    nc = tc.nc
    with ExitStack() as ctx:
        consts = ctx.enter_context(tc.tile_pool(name="consts", bufs=1))
        q_pool = ctx.enter_context(tc.tile_pool(name="q_pool", bufs=GROUPS))
        kv_pool = ctx.enter_context(tc.tile_pool(name="kv_pool", bufs=WINDOWS))
        short = ctx.enter_context(tc.tile_pool(name="short", bufs=3 * UNIT_BANKS))
        waiting = ctx.enter_context(tc.tile_pool(name="waiting", bufs=MX_LAG + 1))
        out_pool = ctx.enter_context(tc.tile_pool(name="out_pool", bufs=UNITS // 2))
        t_psum = ctx.enter_context(tc.psum_pool(name="t_psum", bufs=UNIT_BANKS))
        o_psum = ctx.enter_context(tc.psum_pool(name="o_psum", bufs=UNIT_BANKS))
        r_psum = ctx.enter_context(tc.psum_pool(name="r_psum", bufs=UNIT_ROWS))
        ctx.enter_context(tc.manual_schedule())

        q_rows = q_feat[0].rearrange("h n w d -> h (n w) d")
        out_rows = out[0].rearrange("n w c -> (n w) c")
        q_tiles = []
        kv_tiles = []
        w_raw = consts.tile([P, HEADS, CHANNELS], BF16, name="w_raw")
        bias_rows = consts.tile([P, CHANNELS], BF16, name="bias_rows")
        nc.vector.memset(bias_rows[:], 0.0)
        for g in range(GROUPS):
            q_sb = q_pool.tile([P, HEADS, GROUP_ROWS, HEAD_DIM], BF16, name="q_sb")
            q_group = q_rows[:, g * GROUP_POSITIONS : (g + 1) * GROUP_POSITIONS, :].rearrange(
                "h (p r) d -> p h r d", r=GROUP_ROWS
            )
            if g == 0:
                for u in range(GROUP_UNITS):
                    rows = slice(u * UNIT_ROWS, (u + 1) * UNIT_ROWS)
                    nc.sync.dma_start(out=q_sb[:, :, rows, :], in_=q_group[:, :, rows, :])
            else:
                nc.sync.dma_start(out=q_sb[:], in_=q_group)
            q_tiles.append(q_sb)
            for a in range(GROUP):
                kv_sb = kv_pool.tile([P, HEADS, HEAD_DIM], BF16, name="kv_sb")
                nc.sync.dma_start(out=kv_sb[:], in_=kv_mix[0, :, g * GROUP + a].rearrange("h d e -> d h e"))
                kv_tiles.append(kv_sb)
            if g == 0:
                nc.sync.dma_start(out=w_raw[:], in_=w_out.rearrange("(t e) c -> e t c", e=P))
                nc.sync.dma_start(out=bias_rows[0:1, :], in_=b_out.rearrange("(o c) -> o c", o=1))

        ident = consts.tile([P, P], BF16, name="ident")
        make_identity(nc, ident[:])
        ones = consts.tile([P, P], BF16, name="ones")
        nc.vector.memset(ones[:], 1.0)

        w_codes = consts.tile([P, CHANNELS], U32, name="w_codes", align_bytes=64)
        w_scales = consts.tile([P, CHANNELS], U8, name="w_scales", align_bytes=64)
        bias_sb = consts.tile([P, CHANNELS], F32, name="bias_sb")

        def prepare_projection():
            w_grouped = consts.tile([P, CHANNELS, HEADS], BF16, name="w_grouped", align_bytes=64)
            nc.vector.tensor_copy(out=w_grouped[:], in_=w_raw[:].rearrange("e t c -> e c t"))
            nc.vector.quantize_mx(
                out=w_codes[:].bitcast(FP8X4),
                scales=w_scales[:],
                in_=w_grouped[:].rearrange("e c t -> e (c t)"),
            )
            bias_ps = r_psum.tile([P, CHANNELS], F32, name="bias_ps", tag="r_bank")
            nc.tensor.matmul(out=bias_ps[:], lhsT=ones[:], rhs=bias_rows[:], start=True, stop=True)
            nc.vector.tensor_copy(out=bias_sb[:], in_=bias_ps[:])

        q_transposed = {}
        m_grouped = {}
        m_codes = {}
        m_scales = {}

        def readout(unit, a, h, o_bank):
            qT = q_transposed[unit, h // BANK_HEADS]
            blocks = qT[:].rearrange("d (s j p) -> d s j p", s=BANK_HEADS, j=UNIT_ROWS)
            nc.tensor.matmul(
                out=o_bank[:, h, :, :],
                lhsT=kv_tiles[unit // GROUP_UNITS * GROUP + a][:, h, :],
                rhs=blocks[:, h % BANK_HEADS, :, a * SHARE : (a + 1) * SHARE],
                start=True,
                stop=True,
            )

        def transpose_pair(unit, bank, turn, t_bank):
            for block in range(2 * turn, 2 * turn + 2):
                h = bank * BANK_HEADS + block // UNIT_ROWS
                r = unit % GROUP_UNITS * UNIT_ROWS + block % UNIT_ROWS
                nc.tensor.transpose(
                    t_bank[:, block * P : (block + 1) * P], q_tiles[unit // GROUP_UNITS][:, h, r, :], ident[:]
                )

        def readout_and_transpose(unit_read, unit_next):
            if unit_read is not None:
                grouped = short.tile([P, UNIT_ROWS, P, HEADS], BF16, name="grouped", align_bytes=64)
                m_grouped[unit_read] = grouped
            for bank in range(UNIT_BANKS):
                if unit_read is not None:
                    o_bank = o_psum.tile([P, HEADS, UNIT_ROWS, SHARE], BF16, name="o_bank")
                if unit_next is not None:
                    t_bank = t_psum.tile([P, BANK_BLOCKS * P], BF16, name="t_bank")
                for turn in range(HEADS):
                    if unit_read is not None:
                        readout(unit_read, bank, turn, o_bank)
                    if unit_next is not None:
                        transpose_pair(unit_next, bank, turn, t_bank)
                if unit_next is not None:
                    qT = short.tile([P, BANK_BLOCKS * P], BF16, name="qT")
                    if unit_next < MX_LAG:
                        nc.vector.tensor_copy(out=qT[:].bitcast(F32), in_=t_bank[:].bitcast(F32))
                    else:
                        nc.scalar.copy(out=qT[:].bitcast(F32), in_=t_bank[:].bitcast(F32))
                    q_transposed[unit_next, bank] = qT
                if unit_read is not None:
                    nc.scalar.copy(
                        out=grouped[:, :, bank * SHARE : (bank + 1) * SHARE, :],
                        in_=o_bank[:].rearrange("e t j i -> e j i t"),
                    )

        def quantise_unit(unit):
            codes = waiting.tile([P, UNIT_ROWS * P], U32, name="codes", align_bytes=64)
            scales = waiting.tile([P, UNIT_ROWS * P], U8, name="scales", align_bytes=64)
            nc.vector.quantize_mx(
                out=codes[:].bitcast(FP8X4),
                scales=scales[:],
                in_=m_grouped[unit][:].rearrange("e j p t -> e (j p t)"),
            )
            m_codes[unit] = codes
            m_scales[unit] = scales

        def project_unit(unit):
            g = unit // GROUP_UNITS
            u = unit % GROUP_UNITS
            out_unit = out_rows[g * GROUP_POSITIONS : (g + 1) * GROUP_POSITIONS, :].rearrange(
                "(p r) c -> p r c", r=GROUP_ROWS
            )[:, u * UNIT_ROWS : (u + 1) * UNIT_ROWS, :]
            out_sb = out_pool.tile([P, UNIT_ROWS, CHANNELS], F32, name="out_sb")
            for j in range(UNIT_ROWS):
                r_bank = r_psum.tile([P, CHANNELS], F32, name="r_bank", tag="r_bank")
                nc.tensor.matmul_mx(
                    out=r_bank[:],
                    lhsT=m_codes[unit][:, j * P : (j + 1) * P].bitcast(FP8X4),
                    lhsT_scale=m_scales[unit][:, j * P : (j + 1) * P],
                    rhs=w_codes[:].bitcast(FP8X4),
                    rhs_scale=w_scales[:],
                    start=True,
                    stop=True,
                )
                nc.vector.tensor_tensor(out=out_sb[:, j, :], in0=r_bank[:], in1=bias_sb[:], op=mybir.AluOpType.add)
            nc.sync.dma_start(out=out_unit, in_=out_sb[:])

        for step in range(UNITS + MX_LAG):
            unit_next = step if step < UNITS else None
            unit_read = step - 1 if 1 <= step <= UNITS else None
            if unit_next is not None or unit_read is not None:
                readout_and_transpose(unit_read, unit_next)
            if step == MX_LAG - 1:
                prepare_projection()
            if step >= MX_LAG:
                project_unit(step - MX_LAG)
            if unit_read is not None:
                quantise_unit(unit_read)
